import numpy as np
import ml_dtypes

BF16 = ml_dtypes.bfloat16


def bf(x):
    return np.asarray(x, np.float32).astype(BF16)


def f32(x):
    return np.asarray(x, np.float32)


def f64(x):
    return np.asarray(x).astype(np.float64)


def striped(idx):
    return np.tile(idx.reshape(-1, 16).T, (8, 1))


C, B, S, N = 512, 1024, 1024, 512


def setup_inputs():
    p = 0.2 + 0.6 * np.random.random((1, C))
    label = bf(np.random.random((B, C)) < p)
    u = np.random.random((C, N))
    far = np.random.random((C, N)) < 0.5
    sgn = np.where(np.random.random((C, N)) < 0.5, -1.0, 1.0)
    pre_adj = f32(np.where(far, sgn * (2.1 + 0.9 * u), 0.05 + 0.9 * u))
    base = f32(np.random.standard_normal((C, S)))
    return {"base": base, "pre_adj": pre_adj, "label": label, "offs": striped(np.random.permutation(S)[:N])}


def reference(base, pre_adj, label, offs):
    idx = offs[:16].T.reshape(-1)
    lab = f64(label)
    cooc = lab.T @ lab
    count = lab.sum(axis=0)[:, None]
    r = np.abs(f64(pre_adj) - cooc / count)
    flag = (r < 1.0).astype(np.float64)
    out = f64(base).copy()
    out[:, idx] = flag * r * r + (1.0 - flag) * (r - 0.5)
    return out

@@ -1,0 +1,103 @@
+import concourse.mybir as mybir
+
+F32 = mybir.dt.float32
+BF16 = mybir.dt.bfloat16
+U16 = mybir.dt.uint16
+ALU = mybir.AluOpType
+ACT = mybir.ActivationFunctionType
+
+P = 128
+CLASSES = 512
+SAMPLES = 1024
+SLOTS = 1024
+BLOCKS = CLASSES // P
+STEPS = SAMPLES // P
+STEPS_PER_LOAD = 2
+FLOPS = 2 * SAMPLES * CLASSES * CLASSES
+
+
+def tile_adjloss_kernel(tc, base, pre_adj, label, offs, out):
+    nc = tc.nc
+    with (
+        tc.tile_pool(name="held", bufs=1) as held,
+        tc.tile_pool(name="work", bufs=BLOCKS) as work,
+        tc.psum_pool(name="psum", bufs=BLOCKS) as psum,
+    ):
+        offsets = held.tile([P, CLASSES // 16], U16, name="offsets")
+        nc.sync.dma_start(offsets[:], offs)
+
+        label_by_partition = label.rearrange("(p k) c -> p k c", k=STEPS)
+        samples = []
+        for n in range(STEPS // STEPS_PER_LOAD):
+            piece = held.tile([P, STEPS_PER_LOAD, CLASSES], BF16, name=f"samples{n}")
+            queue = nc.sync if n % 2 == 0 else nc.scalar
+            queue.dma_start(
+                piece[:], label_by_partition[:, n * STEPS_PER_LOAD : (n + 1) * STEPS_PER_LOAD, :]
+            )
+            samples.append(piece)
+
+        predicted = []
+        windows = []
+        for b in range(BLOCKS):
+            block_rows = slice(b * P, (b + 1) * P)
+            predicted.append(held.tile([P, CLASSES], F32, name=f"predicted{b}"))
+            nc.scalar.dma_start(predicted[b][:], pre_adj[block_rows, :])
+            windows.append(held.tile([P, SLOTS], F32, name=f"window{b}"))
+            nc.sync.dma_start(windows[b][:], base[block_rows, :])
+
+        ones = held.tile([P, 1], BF16, name="ones")
+        nc.vector.memset(ones[:], 1.0)
+        minus_half = held.tile([P, 1], F32, name="minus_half")
+        nc.vector.memset(minus_half[:], -0.5)
+
+        def block_of_classes(k, b):
+            return samples[k // STEPS_PER_LOAD][:, k % STEPS_PER_LOAD, b * P : (b + 1) * P]
+
+        def all_classes(k):
+            return samples[k // STEPS_PER_LOAD][:, k % STEPS_PER_LOAD, :]
+
+        def invert_count(b):
+            count = psum.tile([P, 1], F32, name="count")
+            for k in range(STEPS):
+                nc.tensor.matmul(
+                    count[:], block_of_classes(k, b), ones[:], start=(k == 0), stop=(k == STEPS - 1)
+                )
+            inverse = held.tile([P, 1], F32, name=f"inverse_count{b}")
+            nc.vector.reciprocal(inverse[:], count[:])
+            return inverse
+
+        def co_occurrence(b):
+            cooc = psum.tile([P, CLASSES], F32, name="cooc")
+            for k in range(STEPS):
+                nc.tensor.matmul(
+                    cooc[:], block_of_classes(k, b), all_classes(k), start=(k == 0), stop=(k == STEPS - 1)
+                )
+            return cooc
+
+        inverse_counts = [invert_count(0)]
+        coocs = [co_occurrence(0)]
+        for b in range(1, BLOCKS):
+            inverse_counts.append(invert_count(b))
+        for b in range(1, BLOCKS):
+            coocs.append(co_occurrence(b))
+
+        for b in range(BLOCKS):
+            t = work.tile([P, CLASSES], F32, name="t")
+            nc.scalar.activation(t[:], coocs[b][:], ACT.Copy, scale=inverse_counts[b][:])
+            d = work.tile([P, CLASSES], F32, name="d")
+            nc.gpsimd.tensor_tensor(d[:], t[:], predicted[b][:], ALU.subtract)
+            r = work.tile([P, CLASSES], F32, name="r")
+            nc.scalar.activation(r[:], d[:], ACT.Abs)
+            half_sign = work.tile([P, CLASSES], F32, name="half_sign")
+            nc.gpsimd.tensor_scalar(half_sign[:], r[:], 1.0, 0.5, ALU.is_lt, ALU.subtract)
+            signed_r = work.tile([P, CLASSES], F32, name="signed_r")
+            nc.gpsimd.tensor_tensor(signed_r[:], half_sign[:], r[:], ALU.mult)
+            small_r = work.tile([P, CLASSES], F32, name="small_r")
+            nc.scalar.activation(small_r[:], signed_r[:], ACT.Relu, scale=2.0)
+            q = work.tile([P, CLASSES], F32, name="q")
+            nc.scalar.activation(q[:], small_r[:], ACT.Square)
+            l = work.tile([P, CLASSES], F32, name="l")
+            nc.scalar.activation(l[:], signed_r[:], ACT.Relu, bias=minus_half[:], scale=-2.0)
+
+            nc.vector.tensor_tensor(windows[b][:].indirect(offsets[:]), q[:], l[:], ALU.add)
+            nc.sync.dma_start(out[b * P : (b + 1) * P, :], windows[b][:])

@@ -47,6 +47,8 @@ def tile_adjloss_kernel(tc, base, pre_adj, label, offs, out):
 
         ones = held.tile([P, 1], BF16, name="ones")
         nc.vector.memset(ones[:], 1.0)
+        plus_one = held.tile([P, 1], F32, name="plus_one")
+        nc.vector.memset(plus_one[:], 1.0)
         minus_half = held.tile([P, 1], F32, name="minus_half")
         nc.vector.memset(minus_half[:], -0.5)
 
@@ -81,23 +83,29 @@ def tile_adjloss_kernel(tc, base, pre_adj, label, offs, out):
         for b in range(1, BLOCKS):
             coocs.append(co_occurrence(b))
 
-        for b in range(BLOCKS):
-            t = work.tile([P, CLASSES], F32, name="t")
-            nc.scalar.activation(t[:], coocs[b][:], ACT.Copy, scale=inverse_counts[b][:])
+        def losses(b):
             d = work.tile([P, CLASSES], F32, name="d")
-            nc.gpsimd.tensor_tensor(d[:], t[:], predicted[b][:], ALU.subtract)
+            nc.vector.scalar_tensor_tensor(
+                d[:], coocs[b][:], inverse_counts[b][:], predicted[b][:], ALU.mult, ALU.subtract
+            )
             r = work.tile([P, CLASSES], F32, name="r")
             nc.scalar.activation(r[:], d[:], ACT.Abs)
-            half_sign = work.tile([P, CLASSES], F32, name="half_sign")
-            nc.gpsimd.tensor_scalar(half_sign[:], r[:], 1.0, 0.5, ALU.is_lt, ALU.subtract)
-            signed_r = work.tile([P, CLASSES], F32, name="signed_r")
-            nc.gpsimd.tensor_tensor(signed_r[:], half_sign[:], r[:], ALU.mult)
+            y = work.tile([P, CLASSES], F32, name="y")
+            nc.vector.scalar_tensor_tensor(y[:], r[:], 1.0, r[:], ALU.is_lt, ALU.subtract)
+            l = work.tile([P, CLASSES], F32, name="l")
+            nc.scalar.activation(l[:], y[:], ACT.Relu, bias=minus_half[:], scale=-1.0)
+            size_of_y = work.tile([P, CLASSES], F32, name="size_of_y")
+            nc.scalar.activation(size_of_y[:], y[:], ACT.Abs)
             small_r = work.tile([P, CLASSES], F32, name="small_r")
-            nc.scalar.activation(small_r[:], signed_r[:], ACT.Relu, scale=2.0)
+            nc.scalar.activation(small_r[:], size_of_y[:], ACT.Relu, bias=plus_one[:], scale=-1.0)
             q = work.tile([P, CLASSES], F32, name="q")
             nc.scalar.activation(q[:], small_r[:], ACT.Square)
-            l = work.tile([P, CLASSES], F32, name="l")
-            nc.scalar.activation(l[:], signed_r[:], ACT.Relu, bias=minus_half[:], scale=-2.0)
+            return q, l
 
+        ready = losses(0)
+        for b in range(BLOCKS):
+            q, l = ready
+            if b + 1 < BLOCKS:
+                ready = losses(b + 1)
             nc.vector.tensor_tensor(windows[b][:].indirect(offsets[:]), q[:], l[:], ALU.add)
             nc.sync.dma_start(out[b * P : (b + 1) * P, :], windows[b][:])

@@ -89,7 +89,7 @@ def tile_adjloss_kernel(tc, base, pre_adj, label, offs, out):
                 d[:], coocs[b][:], inverse_counts[b][:], predicted[b][:], ALU.mult, ALU.subtract
             )
             r = work.tile([P, CLASSES], F32, name="r")
-            nc.scalar.activation(r[:], d[:], ACT.Abs)
+            nc.vector.scalar_tensor_tensor(r[:], d[:], -1.0, d[:], ALU.mult, ALU.max)
             y = work.tile([P, CLASSES], F32, name="y")
             nc.vector.scalar_tensor_tensor(y[:], r[:], 1.0, r[:], ALU.is_lt, ALU.subtract)
             l = work.tile([P, CLASSES], F32, name="l")
@@ -102,10 +102,10 @@ def tile_adjloss_kernel(tc, base, pre_adj, label, offs, out):
             nc.scalar.activation(q[:], small_r[:], ACT.Square)
             return q, l
 
-        ready = losses(0)
+        summands = losses(0)
         for b in range(BLOCKS):
-            q, l = ready
+            q, l = summands
             if b + 1 < BLOCKS:
-                ready = losses(b + 1)
+                summands = losses(b + 1)
             nc.vector.tensor_tensor(windows[b][:].indirect(offsets[:]), q[:], l[:], ALU.add)
             nc.sync.dma_start(out[b * P : (b + 1) * P, :], windows[b][:])

@@ -12,6 +12,7 @@ SAMPLES = 1024
 SLOTS = 1024
 BLOCKS = CLASSES // P
 STEPS = SAMPLES // P
+HALF = CLASSES // 2
 STEPS_PER_LOAD = 2
 FLOPS = 2 * SAMPLES * CLASSES * CLASSES
 
@@ -21,7 +22,8 @@ def tile_adjloss_kernel(tc, base, pre_adj, label, offs, out):
     with (
         tc.tile_pool(name="held", bufs=1) as held,
         tc.tile_pool(name="work", bufs=BLOCKS) as work,
-        tc.psum_pool(name="psum", bufs=BLOCKS) as psum,
+        tc.psum_pool(name="counts", bufs=2) as counts,
+        tc.psum_pool(name="products", bufs=2) as products,
     ):
         offsets = held.tile([P, CLASSES // 16], U16, name="offsets")
         nc.sync.dma_start(offsets[:], offs)
@@ -51,15 +53,17 @@ def tile_adjloss_kernel(tc, base, pre_adj, label, offs, out):
         nc.vector.memset(plus_one[:], 1.0)
         minus_half = held.tile([P, 1], F32, name="minus_half")
         nc.vector.memset(minus_half[:], -0.5)
+        table_warmer = held.tile([P, 1], F32, name="table_warmer")
+        nc.scalar.activation(table_warmer[:], plus_one[:], ACT.Relu)
 
         def block_of_classes(k, b):
             return samples[k // STEPS_PER_LOAD][:, k % STEPS_PER_LOAD, b * P : (b + 1) * P]
 
-        def all_classes(k):
-            return samples[k // STEPS_PER_LOAD][:, k % STEPS_PER_LOAD, :]
+        def half_of_classes(k, h):
+            return samples[k // STEPS_PER_LOAD][:, k % STEPS_PER_LOAD, h * HALF : (h + 1) * HALF]
 
         def invert_count(b):
-            count = psum.tile([P, 1], F32, name="count")
+            count = counts.tile([P, 1], F32, name="count")
             for k in range(STEPS):
                 nc.tensor.matmul(
                     count[:], block_of_classes(k, b), ones[:], start=(k == 0), stop=(k == STEPS - 1)
@@ -69,11 +73,16 @@ def tile_adjloss_kernel(tc, base, pre_adj, label, offs, out):
             return inverse
 
         def co_occurrence(b):
-            cooc = psum.tile([P, CLASSES], F32, name="cooc")
+            cooc = [products.tile([P, HALF], F32, name=f"cooc{h}") for h in range(2)]
             for k in range(STEPS):
-                nc.tensor.matmul(
-                    cooc[:], block_of_classes(k, b), all_classes(k), start=(k == 0), stop=(k == STEPS - 1)
-                )
+                for h in range(2):
+                    nc.tensor.matmul(
+                        cooc[h][:],
+                        block_of_classes(k, b),
+                        half_of_classes(k, h),
+                        start=(k == 0),
+                        stop=(k == STEPS - 1),
+                    )
             return cooc
 
         inverse_counts = [invert_count(0)]
@@ -83,23 +92,36 @@ def tile_adjloss_kernel(tc, base, pre_adj, label, offs, out):
         for b in range(1, BLOCKS):
             coocs.append(co_occurrence(b))
 
+        def halves(name):
+            return [work.tile([P, HALF], F32, name=f"{name}{h}") for h in range(2)]
+
         def losses(b):
-            d = work.tile([P, CLASSES], F32, name="d")
-            nc.vector.scalar_tensor_tensor(
-                d[:], coocs[b][:], inverse_counts[b][:], predicted[b][:], ALU.mult, ALU.subtract
-            )
-            r = work.tile([P, CLASSES], F32, name="r")
-            nc.vector.scalar_tensor_tensor(r[:], d[:], -1.0, d[:], ALU.mult, ALU.max)
-            y = work.tile([P, CLASSES], F32, name="y")
-            nc.vector.scalar_tensor_tensor(y[:], r[:], 1.0, r[:], ALU.is_lt, ALU.subtract)
-            l = work.tile([P, CLASSES], F32, name="l")
-            nc.scalar.activation(l[:], y[:], ACT.Relu, bias=minus_half[:], scale=-1.0)
-            size_of_y = work.tile([P, CLASSES], F32, name="size_of_y")
-            nc.scalar.activation(size_of_y[:], y[:], ACT.Abs)
-            small_r = work.tile([P, CLASSES], F32, name="small_r")
-            nc.scalar.activation(small_r[:], size_of_y[:], ACT.Relu, bias=plus_one[:], scale=-1.0)
+            d, r, y, size_of_y, small_r = halves("d"), halves("r"), halves("y"), halves("size_of_y"), halves("small_r")
             q = work.tile([P, CLASSES], F32, name="q")
-            nc.scalar.activation(q[:], small_r[:], ACT.Square)
+            l = work.tile([P, CLASSES], F32, name="l")
+            for h in range(2):
+                nc.vector.scalar_tensor_tensor(
+                    d[h][:],
+                    coocs[b][h][:],
+                    inverse_counts[b][:],
+                    predicted[b][:, h * HALF : (h + 1) * HALF],
+                    ALU.mult,
+                    ALU.subtract,
+                )
+            for h in range(2):
+                nc.vector.scalar_tensor_tensor(r[h][:], d[h][:], -1.0, d[h][:], ALU.mult, ALU.max)
+            for h in range(2):
+                nc.vector.scalar_tensor_tensor(y[h][:], r[h][:], 1.0, r[h][:], ALU.is_lt, ALU.subtract)
+            for h in range(2):
+                nc.scalar.activation(size_of_y[h][:], y[h][:], ACT.Abs)
+            for h in range(2):
+                nc.scalar.activation(small_r[h][:], size_of_y[h][:], ACT.Relu, bias=plus_one[:], scale=-1.0)
+            for h in range(2):
+                nc.scalar.activation(q[:, h * HALF : (h + 1) * HALF], small_r[h][:], ACT.Square)
+            for h in range(2):
+                nc.scalar.activation(
+                    l[:, h * HALF : (h + 1) * HALF], y[h][:], ACT.Relu, bias=minus_half[:], scale=-1.0
+                )
             return q, l
 
         summands = losses(0)

@@ -3,6 +3,7 @@ import concourse.mybir as mybir
 F32 = mybir.dt.float32
 BF16 = mybir.dt.bfloat16
 U16 = mybir.dt.uint16
+I32 = mybir.dt.int32
 ALU = mybir.AluOpType
 ACT = mybir.ActivationFunctionType
 
@@ -14,6 +15,7 @@ BLOCKS = CLASSES // P
 STEPS = SAMPLES // P
 HALF = CLASSES // 2
 STEPS_PER_LOAD = 2
+ALL_BUT_SIGN = 0x7FFFFFFF
 FLOPS = 2 * SAMPLES * CLASSES * CLASSES
 
 
@@ -109,7 +111,9 @@ def tile_adjloss_kernel(tc, base, pre_adj, label, offs, out):
                     ALU.subtract,
                 )
             for h in range(2):
-                nc.vector.scalar_tensor_tensor(r[h][:], d[h][:], -1.0, d[h][:], ALU.mult, ALU.max)
+                nc.vector.tensor_scalar(
+                    r[h][:].bitcast(I32), d[h][:].bitcast(I32), ALL_BUT_SIGN, None, ALU.bitwise_and
+                )
             for h in range(2):
                 nc.vector.scalar_tensor_tensor(y[h][:], r[h][:], 1.0, r[h][:], ALU.is_lt, ALU.subtract)
             for h in range(2):

@@ -16,6 +16,7 @@ STEPS = SAMPLES // P
 HALF = CLASSES // 2
 STEPS_PER_LOAD = 2
 ALL_BUT_SIGN = 0x7FFFFFFF
+WARM_UP = 6
 FLOPS = 2 * SAMPLES * CLASSES * CLASSES
 
 
@@ -51,6 +52,8 @@ def tile_adjloss_kernel(tc, base, pre_adj, label, offs, out):
 
         ones = held.tile([P, 1], BF16, name="ones")
         nc.vector.memset(ones[:], 1.0)
+        zeros = held.tile([P, HALF], BF16, name="zeros")
+        nc.vector.memset(zeros[:], 0.0)
         plus_one = held.tile([P, 1], F32, name="plus_one")
         nc.vector.memset(plus_one[:], 1.0)
         minus_half = held.tile([P, 1], F32, name="minus_half")
@@ -74,25 +77,28 @@ def tile_adjloss_kernel(tc, base, pre_adj, label, offs, out):
             nc.vector.reciprocal(inverse[:], count[:])
             return inverse
 
-        def co_occurrence(b):
+        def co_occurrence(b, warm_up):
             cooc = [products.tile([P, HALF], F32, name=f"cooc{h}") for h in range(2)]
+            for n in range(warm_up):
+                for h in range(2):
+                    nc.tensor.matmul(cooc[h][:], zeros[:, 0:P], zeros[:], start=(n == 0), stop=False)
             for k in range(STEPS):
                 for h in range(2):
                     nc.tensor.matmul(
                         cooc[h][:],
                         block_of_classes(k, b),
                         half_of_classes(k, h),
-                        start=(k == 0),
+                        start=(warm_up == 0 and k == 0),
                         stop=(k == STEPS - 1),
                     )
             return cooc
 
         inverse_counts = [invert_count(0)]
-        coocs = [co_occurrence(0)]
+        coocs = [co_occurrence(0, WARM_UP)]
         for b in range(1, BLOCKS):
             inverse_counts.append(invert_count(b))
         for b in range(1, BLOCKS):
-            coocs.append(co_occurrence(b))
+            coocs.append(co_occurrence(b, 0))
 
         def halves(name):
             return [work.tile([P, HALF], F32, name=f"{name}{h}") for h in range(2)]

@@ -1,9 +1,9 @@
 import concourse.mybir as mybir
+from concourse.masks import make_identity
 
 F32 = mybir.dt.float32
 BF16 = mybir.dt.bfloat16
 U16 = mybir.dt.uint16
-I32 = mybir.dt.int32
 ALU = mybir.AluOpType
 ACT = mybir.ActivationFunctionType
 
@@ -15,7 +15,7 @@ BLOCKS = CLASSES // P
 STEPS = SAMPLES // P
 HALF = CLASSES // 2
 STEPS_PER_LOAD = 2
-ALL_BUT_SIGN = 0x7FFFFFFF
+BLOCKS_BY_VECTOR = 1
 WARM_UP = 6
 FLOPS = 2 * SAMPLES * CLASSES * CLASSES
 
@@ -25,7 +25,7 @@ def tile_adjloss_kernel(tc, base, pre_adj, label, offs, out):
     with (
         tc.tile_pool(name="held", bufs=1) as held,
         tc.tile_pool(name="work", bufs=BLOCKS) as work,
-        tc.psum_pool(name="counts", bufs=2) as counts,
+        tc.psum_pool(name="counts", bufs=BLOCKS) as counts,
         tc.psum_pool(name="products", bufs=2) as products,
     ):
         offsets = held.tile([P, CLASSES // 16], U16, name="offsets")
@@ -58,6 +58,8 @@ def tile_adjloss_kernel(tc, base, pre_adj, label, offs, out):
         nc.vector.memset(plus_one[:], 1.0)
         minus_half = held.tile([P, 1], F32, name="minus_half")
         nc.vector.memset(minus_half[:], -0.5)
+        identity = held.tile([P, P], F32, name="identity")
+        make_identity(nc, identity[:])
         table_warmer = held.tile([P, 1], F32, name="table_warmer")
         nc.scalar.activation(table_warmer[:], plus_one[:], ACT.Relu)
 
@@ -67,6 +69,10 @@ def tile_adjloss_kernel(tc, base, pre_adj, label, offs, out):
         def half_of_classes(k, h):
             return samples[k // STEPS_PER_LOAD][:, k % STEPS_PER_LOAD, h * HALF : (h + 1) * HALF]
 
+        minus_counts = {
+            b: held.tile([P, P], F32, name=f"minus_count{b}") for b in range(BLOCKS_BY_VECTOR, BLOCKS)
+        }
+
         def invert_count(b):
             count = counts.tile([P, 1], F32, name="count")
             for k in range(STEPS):
@@ -75,6 +81,8 @@ def tile_adjloss_kernel(tc, base, pre_adj, label, offs, out):
                 )
             inverse = held.tile([P, 1], F32, name=f"inverse_count{b}")
             nc.vector.reciprocal(inverse[:], count[:])
+            if b >= BLOCKS_BY_VECTOR:
+                nc.vector.tensor_scalar(minus_counts[b][:], identity[:], count[:], -1.0, ALU.mult, ALU.mult)
             return inverse
 
         def co_occurrence(b, warm_up):
@@ -89,14 +97,21 @@ def tile_adjloss_kernel(tc, base, pre_adj, label, offs, out):
                         block_of_classes(k, b),
                         half_of_classes(k, h),
                         start=(warm_up == 0 and k == 0),
-                        stop=(k == STEPS - 1),
+                        stop=(k == STEPS - 1 and b < BLOCKS_BY_VECTOR),
+                    )
+            if b >= BLOCKS_BY_VECTOR:
+                for h in range(2):
+                    nc.tensor.matmul(
+                        cooc[h][:],
+                        minus_counts[b][:],
+                        predicted[b][:, h * HALF : (h + 1) * HALF],
+                        start=False,
+                        stop=True,
                     )
             return cooc
 
-        inverse_counts = [invert_count(0)]
+        inverse_counts = [invert_count(b) for b in range(BLOCKS)]
         coocs = [co_occurrence(0, WARM_UP)]
-        for b in range(1, BLOCKS):
-            inverse_counts.append(invert_count(b))
         for b in range(1, BLOCKS):
             coocs.append(co_occurrence(b, 0))
 
@@ -104,40 +119,38 @@ def tile_adjloss_kernel(tc, base, pre_adj, label, offs, out):
             return [work.tile([P, HALF], F32, name=f"{name}{h}") for h in range(2)]
 
         def losses(b):
-            d, r, y, size_of_y, small_r = halves("d"), halves("r"), halves("y"), halves("size_of_y"), halves("small_r")
+            r, r_squared, r_less_half = halves("r"), halves("r_squared"), halves("r_less_half")
             q = work.tile([P, CLASSES], F32, name="q")
             l = work.tile([P, CLASSES], F32, name="l")
+            if b < BLOCKS_BY_VECTOR:
+                difference, scale = halves("d"), 1.0
+                for h in range(2):
+                    nc.vector.scalar_tensor_tensor(
+                        difference[h][:],
+                        coocs[b][h][:],
+                        inverse_counts[b][:],
+                        predicted[b][:, h * HALF : (h + 1) * HALF],
+                        ALU.mult,
+                        ALU.subtract,
+                    )
+            else:
+                difference, scale = coocs[b], inverse_counts[b][:]
+            for h in range(2):
+                nc.scalar.activation(r[h][:], difference[h][:], ACT.Abs, scale=scale)
+                nc.scalar.activation(r_squared[h][:], difference[h][:], ACT.Square, scale=scale)
+            for h in range(2):
+                nc.scalar.activation(r_less_half[h][:], r[h][:], ACT.Identity, bias=minus_half[:])
             for h in range(2):
                 nc.vector.scalar_tensor_tensor(
-                    d[h][:],
-                    coocs[b][h][:],
-                    inverse_counts[b][:],
-                    predicted[b][:, h * HALF : (h + 1) * HALF],
-                    ALU.mult,
-                    ALU.subtract,
+                    q[:, h * HALF : (h + 1) * HALF], r[h][:], 1.0, r_squared[h][:], ALU.is_lt, ALU.mult
                 )
             for h in range(2):
-                nc.vector.tensor_scalar(
-                    r[h][:].bitcast(I32), d[h][:].bitcast(I32), ALL_BUT_SIGN, None, ALU.bitwise_and
-                )
-            for h in range(2):
-                nc.vector.scalar_tensor_tensor(y[h][:], r[h][:], 1.0, r[h][:], ALU.is_lt, ALU.subtract)
-            for h in range(2):
-                nc.scalar.activation(size_of_y[h][:], y[h][:], ACT.Abs)
-            for h in range(2):
-                nc.scalar.activation(small_r[h][:], size_of_y[h][:], ACT.Relu, bias=plus_one[:], scale=-1.0)
-            for h in range(2):
-                nc.scalar.activation(q[:, h * HALF : (h + 1) * HALF], small_r[h][:], ACT.Square)
-            for h in range(2):
-                nc.scalar.activation(
-                    l[:, h * HALF : (h + 1) * HALF], y[h][:], ACT.Relu, bias=minus_half[:], scale=-1.0
+                nc.vector.scalar_tensor_tensor(
+                    l[:, h * HALF : (h + 1) * HALF], r[h][:], 1.0, r_less_half[h][:], ALU.is_ge, ALU.mult
                 )
             return q, l
 
-        summands = losses(0)
         for b in range(BLOCKS):
-            q, l = summands
-            if b + 1 < BLOCKS:
-                summands = losses(b + 1)
+            q, l = losses(b)
             nc.vector.tensor_tensor(windows[b][:].indirect(offsets[:]), q[:], l[:], ALU.add)
             nc.sync.dma_start(out[b * P : (b + 1) * P, :], windows[b][:])

@@ -25,7 +25,7 @@ def tile_adjloss_kernel(tc, base, pre_adj, label, offs, out):
     with (
         tc.tile_pool(name="held", bufs=1) as held,
         tc.tile_pool(name="work", bufs=BLOCKS) as work,
-        tc.psum_pool(name="counts", bufs=BLOCKS) as counts,
+        tc.psum_pool(name="counts", bufs=1) as counts,
         tc.psum_pool(name="products", bufs=2) as products,
     ):
         offsets = held.tile([P, CLASSES // 16], U16, name="offsets")
@@ -69,29 +69,28 @@ def tile_adjloss_kernel(tc, base, pre_adj, label, offs, out):
         def half_of_classes(k, h):
             return samples[k // STEPS_PER_LOAD][:, k % STEPS_PER_LOAD, h * HALF : (h + 1) * HALF]
 
-        minus_counts = {
-            b: held.tile([P, P], F32, name=f"minus_count{b}") for b in range(BLOCKS_BY_VECTOR, BLOCKS)
-        }
-
-        def invert_count(b):
-            count = counts.tile([P, 1], F32, name="count")
+        count = counts.tile([P, BLOCKS], F32, name="count")
+        for b in range(BLOCKS):
             for k in range(STEPS):
                 nc.tensor.matmul(
-                    count[:], block_of_classes(k, b), ones[:], start=(k == 0), stop=(k == STEPS - 1)
+                    count[:, b : b + 1], block_of_classes(k, b), ones[:], start=(k == 0), stop=(k == STEPS - 1)
                 )
-            inverse = held.tile([P, 1], F32, name=f"inverse_count{b}")
-            nc.vector.reciprocal(inverse[:], count[:])
-            if b >= BLOCKS_BY_VECTOR:
-                nc.vector.tensor_scalar(minus_counts[b][:], identity[:], count[:], -1.0, ALU.mult, ALU.mult)
-            return inverse
+        inverse_counts = held.tile([P, BLOCKS], F32, name="inverse_counts")
+        nc.vector.reciprocal(inverse_counts[:], count[:])
+        minus_counts = held.tile([P, BLOCKS], F32, name="minus_counts")
+        nc.scalar.activation(minus_counts[:], count[:], ACT.Copy, scale=-1.0)
+        scaled = {}
+        for b in range(BLOCKS_BY_VECTOR, BLOCKS):
+            scaled[b] = held.tile([P, CLASSES], F32, name=f"scaled{b}")
+            nc.gpsimd.tensor_scalar(scaled[b][:], predicted[b][:], minus_counts[:, b : b + 1], None, ALU.mult)
 
         def co_occurrence(b, warm_up):
             cooc = [products.tile([P, HALF], F32, name=f"cooc{h}") for h in range(2)]
             for n in range(warm_up):
                 for h in range(2):
                     nc.tensor.matmul(cooc[h][:], zeros[:, 0:P], zeros[:], start=(n == 0), stop=False)
-            for k in range(STEPS):
-                for h in range(2):
+            for h in range(2):
+                for k in range(STEPS):
                     nc.tensor.matmul(
                         cooc[h][:],
                         block_of_classes(k, b),
@@ -103,14 +102,13 @@ def tile_adjloss_kernel(tc, base, pre_adj, label, offs, out):
                 for h in range(2):
                     nc.tensor.matmul(
                         cooc[h][:],
-                        minus_counts[b][:],
-                        predicted[b][:, h * HALF : (h + 1) * HALF],
+                        identity[:],
+                        scaled[b][:, h * HALF : (h + 1) * HALF],
                         start=False,
                         stop=True,
                     )
             return cooc
 
-        inverse_counts = [invert_count(b) for b in range(BLOCKS)]
         coocs = [co_occurrence(0, WARM_UP)]
         for b in range(1, BLOCKS):
             coocs.append(co_occurrence(b, 0))
@@ -128,13 +126,13 @@ def tile_adjloss_kernel(tc, base, pre_adj, label, offs, out):
                     nc.vector.scalar_tensor_tensor(
                         difference[h][:],
                         coocs[b][h][:],
-                        inverse_counts[b][:],
+                        inverse_counts[:, b : b + 1],
                         predicted[b][:, h * HALF : (h + 1) * HALF],
                         ALU.mult,
                         ALU.subtract,
                     )
             else:
-                difference, scale = coocs[b], inverse_counts[b][:]
+                difference, scale = coocs[b], inverse_counts[:, b : b + 1]
             for h in range(2):
                 nc.scalar.activation(r[h][:], difference[h][:], ACT.Abs, scale=scale)
                 nc.scalar.activation(r_squared[h][:], difference[h][:], ACT.Square, scale=scale)

@@ -79,10 +79,12 @@ def tile_adjloss_kernel(tc, base, pre_adj, label, offs, out):
         nc.vector.reciprocal(inverse_counts[:], count[:])
         minus_counts = held.tile([P, BLOCKS], F32, name="minus_counts")
         nc.scalar.activation(minus_counts[:], count[:], ACT.Copy, scale=-1.0)
-        scaled = {}
+        minus_count_diagonals = {}
         for b in range(BLOCKS_BY_VECTOR, BLOCKS):
-            scaled[b] = held.tile([P, CLASSES], F32, name=f"scaled{b}")
-            nc.gpsimd.tensor_scalar(scaled[b][:], predicted[b][:], minus_counts[:, b : b + 1], None, ALU.mult)
+            minus_count_diagonals[b] = held.tile([P, P], F32, name=f"minus_count_diagonal{b}")
+            nc.scalar.activation(
+                minus_count_diagonals[b][:], identity[:], ACT.Identity, scale=minus_counts[:, b : b + 1]
+            )
 
         def co_occurrence(b, warm_up):
             cooc = [products.tile([P, HALF], F32, name=f"cooc{h}") for h in range(2)]
@@ -102,8 +104,8 @@ def tile_adjloss_kernel(tc, base, pre_adj, label, offs, out):
                 for h in range(2):
                     nc.tensor.matmul(
                         cooc[h][:],
-                        identity[:],
-                        scaled[b][:, h * HALF : (h + 1) * HALF],
+                        minus_count_diagonals[b][:],
+                        predicted[b][:, h * HALF : (h + 1) * HALF],
                         start=False,
                         stop=True,
                     )

@@ -13,7 +13,8 @@ SAMPLES = 1024
 SLOTS = 1024
 BLOCKS = CLASSES // P
 STEPS = SAMPLES // P
-HALF = CLASSES // 2
+PARTS = 4
+WIDTH = CLASSES // PARTS
 STEPS_PER_LOAD = 2
 BLOCKS_BY_VECTOR = 1
 WARM_UP = 6
@@ -26,7 +27,7 @@ def tile_adjloss_kernel(tc, base, pre_adj, label, offs, out):
         tc.tile_pool(name="held", bufs=1) as held,
         tc.tile_pool(name="work", bufs=BLOCKS) as work,
         tc.psum_pool(name="counts", bufs=1) as counts,
-        tc.psum_pool(name="products", bufs=2) as products,
+        tc.psum_pool(name="products", bufs=1) as products,
     ):
         offsets = held.tile([P, CLASSES // 16], U16, name="offsets")
         nc.sync.dma_start(offsets[:], offs)
@@ -52,7 +53,7 @@ def tile_adjloss_kernel(tc, base, pre_adj, label, offs, out):
 
         ones = held.tile([P, 1], BF16, name="ones")
         nc.vector.memset(ones[:], 1.0)
-        zeros = held.tile([P, HALF], BF16, name="zeros")
+        zeros = held.tile([P, P], BF16, name="zeros")
         nc.vector.memset(zeros[:], 0.0)
         plus_one = held.tile([P, 1], F32, name="plus_one")
         nc.vector.memset(plus_one[:], 1.0)
@@ -63,11 +64,14 @@ def tile_adjloss_kernel(tc, base, pre_adj, label, offs, out):
         table_warmer = held.tile([P, 1], F32, name="table_warmer")
         nc.scalar.activation(table_warmer[:], plus_one[:], ACT.Relu)
 
+        def columns(part):
+            return slice(part * WIDTH, (part + 1) * WIDTH)
+
         def block_of_classes(k, b):
             return samples[k // STEPS_PER_LOAD][:, k % STEPS_PER_LOAD, b * P : (b + 1) * P]
 
-        def half_of_classes(k, h):
-            return samples[k // STEPS_PER_LOAD][:, k % STEPS_PER_LOAD, h * HALF : (h + 1) * HALF]
+        def part_of_classes(k, part):
+            return samples[k // STEPS_PER_LOAD][:, k % STEPS_PER_LOAD, columns(part)]
 
         count = counts.tile([P, BLOCKS], F32, name="count")
         for b in range(BLOCKS):
@@ -87,70 +91,60 @@ def tile_adjloss_kernel(tc, base, pre_adj, label, offs, out):
             )
 
         def co_occurrence(b, warm_up):
-            cooc = [products.tile([P, HALF], F32, name=f"cooc{h}") for h in range(2)]
+            cooc = [products.tile([P, WIDTH], F32, name=f"cooc{part}") for part in range(PARTS)]
             for n in range(warm_up):
-                for h in range(2):
-                    nc.tensor.matmul(cooc[h][:], zeros[:, 0:P], zeros[:], start=(n == 0), stop=False)
-            for h in range(2):
+                for part in range(PARTS):
+                    nc.tensor.matmul(cooc[part][:], zeros[:], zeros[:, 0:WIDTH], start=(n == 0), stop=False)
+            for part in range(PARTS):
                 for k in range(STEPS):
                     nc.tensor.matmul(
-                        cooc[h][:],
+                        cooc[part][:],
                         block_of_classes(k, b),
-                        half_of_classes(k, h),
+                        part_of_classes(k, part),
                         start=(warm_up == 0 and k == 0),
                         stop=(k == STEPS - 1 and b < BLOCKS_BY_VECTOR),
                     )
-            if b >= BLOCKS_BY_VECTOR:
-                for h in range(2):
+                if b >= BLOCKS_BY_VECTOR:
                     nc.tensor.matmul(
-                        cooc[h][:],
+                        cooc[part][:],
                         minus_count_diagonals[b][:],
-                        predicted[b][:, h * HALF : (h + 1) * HALF],
+                        predicted[b][:, columns(part)],
                         start=False,
                         stop=True,
                     )
             return cooc
 
-        coocs = [co_occurrence(0, WARM_UP)]
-        for b in range(1, BLOCKS):
-            coocs.append(co_occurrence(b, 0))
-
-        def halves(name):
-            return [work.tile([P, HALF], F32, name=f"{name}{h}") for h in range(2)]
-
-        def losses(b):
-            r, r_squared, r_less_half = halves("r"), halves("r_squared"), halves("r_less_half")
+        def losses(b, cooc):
+            r = work.tile([P, CLASSES], F32, name="r")
+            r_squared = work.tile([P, CLASSES], F32, name="r_squared")
+            r_less_half = work.tile([P, CLASSES], F32, name="r_less_half")
             q = work.tile([P, CLASSES], F32, name="q")
             l = work.tile([P, CLASSES], F32, name="l")
             if b < BLOCKS_BY_VECTOR:
-                difference, scale = halves("d"), 1.0
-                for h in range(2):
+                d = work.tile([P, CLASSES], F32, name="d")
+            for part in range(PARTS):
+                if b < BLOCKS_BY_VECTOR:
                     nc.vector.scalar_tensor_tensor(
-                        difference[h][:],
-                        coocs[b][h][:],
+                        d[:, columns(part)],
+                        cooc[part][:],
                         inverse_counts[:, b : b + 1],
-                        predicted[b][:, h * HALF : (h + 1) * HALF],
+                        predicted[b][:, columns(part)],
                         ALU.mult,
                         ALU.subtract,
                     )
-            else:
-                difference, scale = coocs[b], inverse_counts[:, b : b + 1]
-            for h in range(2):
-                nc.scalar.activation(r[h][:], difference[h][:], ACT.Abs, scale=scale)
-                nc.scalar.activation(r_squared[h][:], difference[h][:], ACT.Square, scale=scale)
-            for h in range(2):
-                nc.scalar.activation(r_less_half[h][:], r[h][:], ACT.Identity, bias=minus_half[:])
-            for h in range(2):
-                nc.vector.scalar_tensor_tensor(
-                    q[:, h * HALF : (h + 1) * HALF], r[h][:], 1.0, r_squared[h][:], ALU.is_lt, ALU.mult
-                )
-            for h in range(2):
-                nc.vector.scalar_tensor_tensor(
-                    l[:, h * HALF : (h + 1) * HALF], r[h][:], 1.0, r_less_half[h][:], ALU.is_ge, ALU.mult
-                )
+                    difference, scale = d[:, columns(part)], 1.0
+                else:
+                    difference, scale = cooc[part][:], inverse_counts[:, b : b + 1]
+                nc.scalar.activation(r[:, columns(part)], difference, ACT.Abs, scale=scale)
+                nc.scalar.activation(r_squared[:, columns(part)], difference, ACT.Square, scale=scale)
+                nc.scalar.activation(r_less_half[:, columns(part)], r[:, columns(part)], ACT.Identity, bias=minus_half[:])
+            steps = [columns(part) for part in range(PARTS)] if b == 0 else [slice(0, CLASSES)]
+            for step in steps:
+                nc.vector.scalar_tensor_tensor(q[:, step], r[:, step], 1.0, r_squared[:, step], ALU.is_lt, ALU.mult)
+                nc.vector.scalar_tensor_tensor(l[:, step], r[:, step], 1.0, r_less_half[:, step], ALU.is_ge, ALU.mult)
             return q, l
 
         for b in range(BLOCKS):
-            q, l = losses(b)
+            q, l = losses(b, co_occurrence(b, WARM_UP if b == 0 else 0))
             nc.vector.tensor_tensor(windows[b][:].indirect(offsets[:]), q[:], l[:], ALU.add)
             nc.sync.dma_start(out[b * P : (b + 1) * P, :], windows[b][:])

@@ -29,9 +29,6 @@ def tile_adjloss_kernel(tc, base, pre_adj, label, offs, out):
         tc.psum_pool(name="counts", bufs=1) as counts,
         tc.psum_pool(name="products", bufs=1) as products,
     ):
-        offsets = held.tile([P, CLASSES // 16], U16, name="offsets")
-        nc.sync.dma_start(offsets[:], offs)
-
         label_by_partition = label.rearrange("(p k) c -> p k c", k=STEPS)
         samples = []
         for n in range(STEPS // STEPS_PER_LOAD):
@@ -41,6 +38,9 @@ def tile_adjloss_kernel(tc, base, pre_adj, label, offs, out):
                 piece[:], label_by_partition[:, n * STEPS_PER_LOAD : (n + 1) * STEPS_PER_LOAD, :]
             )
             samples.append(piece)
+
+        offsets = held.tile([P, CLASSES // 16], U16, name="offsets")
+        nc.sync.dma_start(offsets[:], offs)
 
         predicted = []
         windows = []

@@ -55,14 +55,10 @@ def tile_adjloss_kernel(tc, base, pre_adj, label, offs, out):
         nc.vector.memset(ones[:], 1.0)
         zeros = held.tile([P, P], BF16, name="zeros")
         nc.vector.memset(zeros[:], 0.0)
-        plus_one = held.tile([P, 1], F32, name="plus_one")
-        nc.vector.memset(plus_one[:], 1.0)
         minus_half = held.tile([P, 1], F32, name="minus_half")
         nc.vector.memset(minus_half[:], -0.5)
         identity = held.tile([P, P], F32, name="identity")
         make_identity(nc, identity[:])
-        table_warmer = held.tile([P, 1], F32, name="table_warmer")
-        nc.scalar.activation(table_warmer[:], plus_one[:], ACT.Relu)
 
         def columns(part):
             return slice(part * WIDTH, (part + 1) * WIDTH)

@@ -47,12 +47,14 @@ def tile_adjloss_kernel(tc, base, pre_adj, label, offs, out):
         for b in range(BLOCKS):
             block_rows = slice(b * P, (b + 1) * P)
             predicted.append(held.tile([P, CLASSES], F32, name=f"predicted{b}"))
-            nc.scalar.dma_start(predicted[b][:], pre_adj[block_rows, :])
+            queue = nc.scalar if b == 0 else nc.sync
+            queue.dma_start(predicted[b][:], pre_adj[block_rows, :])
             windows.append(held.tile([P, SLOTS], F32, name=f"window{b}"))
             nc.sync.dma_start(windows[b][:], base[block_rows, :])
 
-        ones = held.tile([P, 1], BF16, name="ones")
-        nc.vector.memset(ones[:], 1.0)
+        pick = held.tile([P, BLOCKS * BLOCKS], BF16, name="pick")
+        nc.vector.memset(pick[:], 0.0)
+        nc.vector.memset(pick[:, :: BLOCKS + 1], 1.0)
         zeros = held.tile([P, P], BF16, name="zeros")
         nc.vector.memset(zeros[:], 0.0)
         minus_half = held.tile([P, 1], F32, name="minus_half")
@@ -70,10 +72,14 @@ def tile_adjloss_kernel(tc, base, pre_adj, label, offs, out):
             return samples[k // STEPS_PER_LOAD][:, k % STEPS_PER_LOAD, columns(part)]
 
         count = counts.tile([P, BLOCKS], F32, name="count")
-        for b in range(BLOCKS):
-            for k in range(STEPS):
+        for k in range(STEPS):
+            for b in range(BLOCKS):
                 nc.tensor.matmul(
-                    count[:, b : b + 1], block_of_classes(k, b), ones[:], start=(k == 0), stop=(k == STEPS - 1)
+                    count[:],
+                    block_of_classes(k, b),
+                    pick[:, b * BLOCKS : (b + 1) * BLOCKS],
+                    start=(k == 0 and b == 0),
+                    stop=(k == STEPS - 1 and b == BLOCKS - 1),
                 )
         inverse_counts = held.tile([P, BLOCKS], F32, name="inverse_counts")
         nc.vector.reciprocal(inverse_counts[:], count[:])

@@ -52,15 +52,16 @@ def tile_adjloss_kernel(tc, base, pre_adj, label, offs, out):
             windows.append(held.tile([P, SLOTS], F32, name=f"window{b}"))
             nc.sync.dma_start(windows[b][:], base[block_rows, :])
 
-        pick = held.tile([P, BLOCKS * BLOCKS], BF16, name="pick")
-        nc.vector.memset(pick[:], 0.0)
-        nc.vector.memset(pick[:, :: BLOCKS + 1], 1.0)
+        ones = held.tile([P, 1], BF16, name="ones")
+        nc.vector.memset(ones[:], 1.0)
         zeros = held.tile([P, P], BF16, name="zeros")
         nc.vector.memset(zeros[:], 0.0)
         minus_half = held.tile([P, 1], F32, name="minus_half")
         nc.vector.memset(minus_half[:], -0.5)
         identity = held.tile([P, P], F32, name="identity")
         make_identity(nc, identity[:])
+        table_loaded = held.tile([P, 1], F32, name="table_loaded")
+        nc.scalar.activation(table_loaded[:], minus_half[:], ACT.Abs)
 
         def columns(part):
             return slice(part * WIDTH, (part + 1) * WIDTH)
@@ -71,26 +72,23 @@ def tile_adjloss_kernel(tc, base, pre_adj, label, offs, out):
         def part_of_classes(k, part):
             return samples[k // STEPS_PER_LOAD][:, k % STEPS_PER_LOAD, columns(part)]
 
-        count = counts.tile([P, BLOCKS], F32, name="count")
-        for k in range(STEPS):
-            for b in range(BLOCKS):
-                nc.tensor.matmul(
-                    count[:],
-                    block_of_classes(k, b),
-                    pick[:, b * BLOCKS : (b + 1) * BLOCKS],
-                    start=(k == 0 and b == 0),
-                    stop=(k == STEPS - 1 and b == BLOCKS - 1),
-                )
-        inverse_counts = held.tile([P, BLOCKS], F32, name="inverse_counts")
-        nc.vector.reciprocal(inverse_counts[:], count[:])
-        minus_counts = held.tile([P, BLOCKS], F32, name="minus_counts")
-        nc.scalar.activation(minus_counts[:], count[:], ACT.Copy, scale=-1.0)
-        minus_count_diagonals = {}
-        for b in range(BLOCKS_BY_VECTOR, BLOCKS):
-            minus_count_diagonals[b] = held.tile([P, P], F32, name=f"minus_count_diagonal{b}")
-            nc.scalar.activation(
-                minus_count_diagonals[b][:], identity[:], ACT.Identity, scale=minus_counts[:, b : b + 1]
-            )
+        def count_classes(name, blocks):
+            count = counts.tile([P, len(blocks)], F32, name=f"count_{name}")
+            for column, b in enumerate(blocks):
+                for k in range(STEPS):
+                    nc.tensor.matmul(
+                        count[:, column : column + 1],
+                        block_of_classes(k, b),
+                        ones[:],
+                        start=(k == 0),
+                        stop=(k == STEPS - 1),
+                    )
+            inverse = held.tile([P, len(blocks)], F32, name=f"inverse_{name}")
+            nc.vector.reciprocal(inverse[:], count[:])
+            return count, inverse
+
+        inverse_first = count_classes("first", [0])[1]
+        inverse_count = {0: inverse_first[:]}
 
         def co_occurrence(b, warm_up):
             cooc = [products.tile([P, WIDTH], F32, name=f"cooc{part}") for part in range(PARTS)]
@@ -129,14 +127,14 @@ def tile_adjloss_kernel(tc, base, pre_adj, label, offs, out):
                     nc.vector.scalar_tensor_tensor(
                         d[:, columns(part)],
                         cooc[part][:],
-                        inverse_counts[:, b : b + 1],
+                        inverse_count[b],
                         predicted[b][:, columns(part)],
                         ALU.mult,
                         ALU.subtract,
                     )
                     difference, scale = d[:, columns(part)], 1.0
                 else:
-                    difference, scale = cooc[part][:], inverse_counts[:, b : b + 1]
+                    difference, scale = cooc[part][:], inverse_count[b]
                 nc.scalar.activation(r[:, columns(part)], difference, ACT.Abs, scale=scale)
                 nc.scalar.activation(r_squared[:, columns(part)], difference, ACT.Square, scale=scale)
                 nc.scalar.activation(r_less_half[:, columns(part)], r[:, columns(part)], ACT.Identity, bias=minus_half[:])
@@ -146,7 +144,25 @@ def tile_adjloss_kernel(tc, base, pre_adj, label, offs, out):
                 nc.vector.scalar_tensor_tensor(l[:, step], r[:, step], 1.0, r_less_half[:, step], ALU.is_ge, ALU.mult)
             return q, l
 
+        minus_count_diagonals = {}
+        later_blocks = list(range(BLOCKS_BY_VECTOR, BLOCKS))
         for b in range(BLOCKS):
-            q, l = losses(b, co_occurrence(b, WARM_UP if b == 0 else 0))
+            cooc = co_occurrence(b, WARM_UP if b == 0 else 0)
+            if b == 0:
+                count_later, inverse_later = count_classes("later", later_blocks)
+                for column, later in enumerate(later_blocks):
+                    inverse_count[later] = inverse_later[:, column : column + 1]
+            q, l = losses(b, cooc)
+            if b == 0:
+                minus_counts = held.tile([P, len(later_blocks)], F32, name="minus_counts")
+                nc.scalar.activation(minus_counts[:], count_later[:], ACT.Copy, scale=-1.0)
+                for column, later in enumerate(later_blocks):
+                    minus_count_diagonals[later] = held.tile([P, P], F32, name=f"minus_count_diagonal{later}")
+                    nc.scalar.activation(
+                        minus_count_diagonals[later][:],
+                        identity[:],
+                        ACT.Identity,
+                        scale=minus_counts[:, column : column + 1],
+                    )
             nc.vector.tensor_tensor(windows[b][:].indirect(offsets[:]), q[:], l[:], ALU.add)
             nc.sync.dma_start(out[b * P : (b + 1) * P, :], windows[b][:])

@@ -12,12 +12,12 @@ CLASSES = 512
 SAMPLES = 1024
 SLOTS = 1024
 BLOCKS = CLASSES // P
+LAST = BLOCKS - 1
 STEPS = SAMPLES // P
-PARTS = 4
-WIDTH = CLASSES // PARTS
 STEPS_PER_LOAD = 2
-BLOCKS_BY_VECTOR = 1
-WARM_UP = 6
+EARLY_STEPS = 4
+PARTS = [4, 2, 2, 2]
+WARM_UP = 5
 FLOPS = 2 * SAMPLES * CLASSES * CLASSES
 
 
@@ -26,8 +26,10 @@ def tile_adjloss_kernel(tc, base, pre_adj, label, offs, out):
     with (
         tc.tile_pool(name="held", bufs=1) as held,
         tc.tile_pool(name="work", bufs=BLOCKS) as work,
+        tc.tile_pool(name="handover", bufs=1) as handover,
         tc.psum_pool(name="counts", bufs=1) as counts,
         tc.psum_pool(name="products", bufs=1) as products,
+        tc.psum_pool(name="wide_products", bufs=2) as wide_products,
     ):
         label_by_partition = label.rearrange("(p k) c -> p k c", k=STEPS)
         samples = []
@@ -58,111 +60,140 @@ def tile_adjloss_kernel(tc, base, pre_adj, label, offs, out):
         nc.vector.memset(zeros[:], 0.0)
         minus_half = held.tile([P, 1], F32, name="minus_half")
         nc.vector.memset(minus_half[:], -0.5)
+        one = held.tile([P, 1], F32, name="one")
+        nc.vector.memset(one[:], 1.0)
         identity = held.tile([P, P], F32, name="identity")
         make_identity(nc, identity[:])
         table_loaded = held.tile([P, 1], F32, name="table_loaded")
         nc.scalar.activation(table_loaded[:], minus_half[:], ACT.Abs)
 
-        def columns(part):
-            return slice(part * WIDTH, (part + 1) * WIDTH)
+        def columns(b, part):
+            width = CLASSES // PARTS[b]
+            return slice(part * width, (part + 1) * width)
 
         def block_of_classes(k, b):
             return samples[k // STEPS_PER_LOAD][:, k % STEPS_PER_LOAD, b * P : (b + 1) * P]
 
-        def part_of_classes(k, part):
-            return samples[k // STEPS_PER_LOAD][:, k % STEPS_PER_LOAD, columns(part)]
+        def add_to_count(count, column, b, steps):
+            for k in steps:
+                nc.tensor.matmul(
+                    count[:, column : column + 1],
+                    block_of_classes(k, b),
+                    ones[:],
+                    start=(k == 0),
+                    stop=(k == STEPS - 1),
+                )
 
-        def count_classes(name, blocks):
-            count = counts.tile([P, len(blocks)], F32, name=f"count_{name}")
-            for column, b in enumerate(blocks):
-                for k in range(STEPS):
-                    nc.tensor.matmul(
-                        count[:, column : column + 1],
-                        block_of_classes(k, b),
-                        ones[:],
-                        start=(k == 0),
-                        stop=(k == STEPS - 1),
-                    )
-            inverse = held.tile([P, len(blocks)], F32, name=f"inverse_{name}")
-            nc.vector.reciprocal(inverse[:], count[:])
-            return count, inverse
+        def add_products(sums, b, part, steps):
+            for k in steps:
+                nc.tensor.matmul(
+                    sums[:],
+                    block_of_classes(k, b),
+                    samples[k // STEPS_PER_LOAD][:, k % STEPS_PER_LOAD, columns(b, part)],
+                    start=(b > 0 and k == 0),
+                    stop=(b == 0 and k == STEPS - 1),
+                )
 
-        inverse_first = count_classes("first", [0])[1]
-        inverse_count = {0: inverse_first[:]}
+        first_width = CLASSES // PARTS[0]
+        first_cooc = [products.tile([P, first_width], F32, name=f"cooc{part}") for part in range(PARTS[0])]
+        for turn in range(WARM_UP):
+            for sums in first_cooc:
+                nc.tensor.matmul(sums[:], zeros[:], zeros[:, 0:first_width], start=(turn == 0), stop=False)
+        count_first = counts.tile([P, 1], F32, name="count_first")
+        for k in range(EARLY_STEPS):
+            add_to_count(count_first, 0, 0, [k])
+            for part, sums in enumerate(first_cooc):
+                add_products(sums, 0, part, [k])
+        late_steps = range(EARLY_STEPS, STEPS)
+        add_to_count(count_first, 0, 0, late_steps)
+        inverse_first = held.tile([P, 1], F32, name="inverse_first")
+        nc.vector.reciprocal(inverse_first[:], count_first[:])
+        for part, sums in enumerate(first_cooc):
+            add_products(sums, 0, part, late_steps)
 
-        def co_occurrence(b, warm_up):
-            cooc = [products.tile([P, WIDTH], F32, name=f"cooc{part}") for part in range(PARTS)]
-            for n in range(warm_up):
-                for part in range(PARTS):
-                    nc.tensor.matmul(cooc[part][:], zeros[:], zeros[:, 0:WIDTH], start=(n == 0), stop=False)
-            for part in range(PARTS):
-                for k in range(STEPS):
-                    nc.tensor.matmul(
-                        cooc[part][:],
-                        block_of_classes(k, b),
-                        part_of_classes(k, part),
-                        start=(warm_up == 0 and k == 0),
-                        stop=(k == STEPS - 1 and b < BLOCKS_BY_VECTOR),
-                    )
-                if b >= BLOCKS_BY_VECTOR:
-                    nc.tensor.matmul(
-                        cooc[part][:],
-                        minus_count_diagonals[b][:],
-                        predicted[b][:, columns(part)],
-                        start=False,
-                        stop=True,
-                    )
-            return cooc
+        count_later = counts.tile([P, BLOCKS - 1], F32, name="count_later")
+        for b in range(1, BLOCKS):
+            add_to_count(count_later, b - 1, b, range(STEPS))
+        inverse_later = held.tile([P, BLOCKS - 1], F32, name="inverse_later")
+        nc.vector.reciprocal(inverse_later[:], count_later[:])
 
-        def losses(b, cooc):
-            r = work.tile([P, CLASSES], F32, name="r")
-            r_squared = work.tile([P, CLASSES], F32, name="r_squared")
-            r_less_half = work.tile([P, CLASSES], F32, name="r_less_half")
-            q = work.tile([P, CLASSES], F32, name="q")
-            l = work.tile([P, CLASSES], F32, name="l")
-            if b < BLOCKS_BY_VECTOR:
-                d = work.tile([P, CLASSES], F32, name="d")
-            for part in range(PARTS):
-                if b < BLOCKS_BY_VECTOR:
-                    nc.vector.scalar_tensor_tensor(
-                        d[:, columns(part)],
-                        cooc[part][:],
-                        inverse_count[b],
-                        predicted[b][:, columns(part)],
-                        ALU.mult,
-                        ALU.subtract,
-                    )
-                    difference, scale = d[:, columns(part)], 1.0
-                else:
-                    difference, scale = cooc[part][:], inverse_count[b]
-                nc.scalar.activation(r[:, columns(part)], difference, ACT.Abs, scale=scale)
-                nc.scalar.activation(r_squared[:, columns(part)], difference, ACT.Square, scale=scale)
-                nc.scalar.activation(r_less_half[:, columns(part)], r[:, columns(part)], ACT.Identity, bias=minus_half[:])
-            steps = [columns(part) for part in range(PARTS)] if b == 0 else [slice(0, CLASSES)]
-            for step in steps:
-                nc.vector.scalar_tensor_tensor(q[:, step], r[:, step], 1.0, r_squared[:, step], ALU.is_lt, ALU.mult)
-                nc.vector.scalar_tensor_tensor(l[:, step], r[:, step], 1.0, r_less_half[:, step], ALU.is_ge, ALU.mult)
-            return q, l
+        def multiply_by_flag(q, r, r_squared, span):
+            nc.vector.scalar_tensor_tensor(q[:, span], r[:, span], 1.0, r_squared[:, span], ALU.is_lt, ALU.mult)
 
-        minus_count_diagonals = {}
-        later_blocks = list(range(BLOCKS_BY_VECTOR, BLOCKS))
-        for b in range(BLOCKS):
-            cooc = co_occurrence(b, WARM_UP if b == 0 else 0)
-            if b == 0:
-                count_later, inverse_later = count_classes("later", later_blocks)
-                for column, later in enumerate(later_blocks):
-                    inverse_count[later] = inverse_later[:, column : column + 1]
-            q, l = losses(b, cooc)
-            if b == 0:
-                minus_counts = held.tile([P, len(later_blocks)], F32, name="minus_counts")
-                nc.scalar.activation(minus_counts[:], count_later[:], ACT.Copy, scale=-1.0)
-                for column, later in enumerate(later_blocks):
-                    minus_count_diagonals[later] = held.tile([P, P], F32, name=f"minus_count_diagonal{later}")
-                    nc.scalar.activation(
-                        minus_count_diagonals[later][:],
-                        identity[:],
-                        ACT.Identity,
-                        scale=minus_counts[:, column : column + 1],
-                    )
+        def multiply_by_no_flag(l, r, r_less_half, span):
+            nc.vector.scalar_tensor_tensor(l[:, span], r[:, span], 1.0, r_less_half[:, span], ALU.is_ge, ALU.mult)
+
+        def place(b, q, l):
             nc.vector.tensor_tensor(windows[b][:].indirect(offsets[:]), q[:], l[:], ALU.add)
             nc.sync.dma_start(out[b * P : (b + 1) * P, :], windows[b][:])
+
+        def new_tile(name):
+            return work.tile([P, CLASSES], F32, name=name)
+
+        d, r, r_squared, r_less_half, q, l = [
+            new_tile(name) for name in ("d", "r", "r_squared", "r_less_half", "q", "l")
+        ]
+        for part, sums in enumerate(first_cooc):
+            span = columns(0, part)
+            nc.vector.scalar_tensor_tensor(
+                d[:, span], sums[:], inverse_first[:], predicted[0][:, span], ALU.mult, ALU.subtract
+            )
+            nc.scalar.activation(r[:, span], d[:, span], ACT.Abs)
+            nc.scalar.activation(r_squared[:, span], d[:, span], ACT.Square)
+            nc.scalar.activation(r_less_half[:, span], r[:, span], ACT.Identity, bias=minus_half[:])
+        for part in range(PARTS[0]):
+            multiply_by_flag(q, r, r_squared, columns(0, part))
+            multiply_by_no_flag(l, r, r_less_half, columns(0, part))
+
+        minus_counts = held.tile([P, BLOCKS - 1], F32, name="minus_counts")
+        nc.scalar.activation(minus_counts[:], count_later[:], ACT.Copy, scale=-1.0)
+        minus_count_diagonals = {}
+        for b in range(1, BLOCKS):
+            minus_count_diagonals[b] = held.tile([P, P], F32, name=f"minus_count_diagonal{b}")
+            nc.scalar.activation(
+                minus_count_diagonals[b][:], identity[:], ACT.Identity, scale=minus_counts[:, b - 1 : b]
+            )
+        place(0, q, l)
+
+        def differences(b):
+            parts = []
+            for part in range(PARTS[b]):
+                sums = wide_products.tile([P, CLASSES // PARTS[b]], F32, name="sums")
+                add_products(sums, b, part, range(STEPS))
+                nc.tensor.matmul(
+                    sums[:], minus_count_diagonals[b][:], predicted[b][:, columns(b, part)], start=False, stop=True
+                )
+                parts.append((columns(b, part), sums))
+            return parts, inverse_later[:, b - 1 : b]
+
+        every_column = slice(0, CLASSES)
+        for b in range(1, LAST):
+            r, r_squared, r_less_half, q = [new_tile(name) for name in ("r", "r_squared", "r_less_half", "q")]
+            parts, inverse_count = differences(b)
+            for span, sums in parts:
+                nc.scalar.activation(r[:, span], sums[:], ACT.Abs, scale=inverse_count)
+            nc.scalar.activation(r_squared[:], r[:], ACT.Square)
+            nc.scalar.activation(r_less_half[:], r[:], ACT.Identity, bias=minus_half[:])
+            multiply_by_flag(q, r, r_squared, every_column)
+            if b < LAST - 1:
+                l = new_tile("l")
+                multiply_by_no_flag(l, r, r_less_half, every_column)
+                place(b, q, l)
+
+        r_last = handover.tile([P, CLASSES], F32, name="r_last", tag="handover")
+        e = new_tile("e")
+        parts, inverse_count = differences(LAST)
+        for span, sums in parts:
+            nc.scalar.activation(r_last[:, span], sums[:], ACT.Abs, scale=inverse_count)
+            nc.vector.scalar_tensor_tensor(e[:, span], r_last[:, span], 1.0, r_last[:, span], ALU.is_lt, ALU.subtract)
+
+        l = handover.tile([P, CLASSES], F32, name="l_before_last", tag="handover")
+        multiply_by_no_flag(l, r, r_less_half, every_column)
+        place(LAST - 1, q, l)
+
+        size_of_e, flagged_r, q, l = [new_tile(name) for name in ("size_of_e", "flagged_r", "q", "l")]
+        nc.scalar.activation(size_of_e[:], e[:], ACT.Abs)
+        nc.scalar.activation(flagged_r[:], size_of_e[:], ACT.Relu, scale=-1.0, bias=one[:])
+        nc.scalar.activation(q[:], flagged_r[:], ACT.Square)
+        nc.scalar.activation(l[:], e[:], ACT.Relu, scale=-1.0, bias=minus_half[:])
+        place(LAST, q, l)

@@ -14,9 +14,9 @@ SLOTS = 1024
 BLOCKS = CLASSES // P
 LAST = BLOCKS - 1
 STEPS = SAMPLES // P
-STEPS_PER_LOAD = 2
-EARLY_STEPS = 4
-PARTS = [4, 2, 2, 2]
+STEPS_PER_LOAD = 4
+EARLY_STEPS = STEPS_PER_LOAD
+WIDTHS = [[128, 128, 128, 128], [256, 256], [256, 256], [384, 128]]
 WARM_UP = 5
 FLOPS = 2 * SAMPLES * CLASSES * CLASSES
 
@@ -34,30 +34,32 @@ def tile_adjloss_kernel(tc, base, pre_adj, label, offs, out):
         label_by_partition = label.rearrange("(p k) c -> p k c", k=STEPS)
         samples = []
         for n in range(STEPS // STEPS_PER_LOAD):
-            piece = held.tile([P, STEPS_PER_LOAD, CLASSES], BF16, name=f"samples{n}")
-            queue = nc.sync if n % 2 == 0 else nc.scalar
-            queue.dma_start(
-                piece[:], label_by_partition[:, n * STEPS_PER_LOAD : (n + 1) * STEPS_PER_LOAD, :]
-            )
-            samples.append(piece)
+            half = held.tile([P, STEPS_PER_LOAD, CLASSES], BF16, name=f"samples{n}")
+            nc.sync.dma_start(half[:], label_by_partition[:, n * STEPS_PER_LOAD : (n + 1) * STEPS_PER_LOAD, :])
+            samples.append(half)
 
+        predicted = [held.tile([P, CLASSES], F32, name=f"predicted{b}") for b in range(BLOCKS)]
+        windows = [held.tile([P, SLOTS], F32, name=f"window{b}") for b in range(BLOCKS)]
         offsets = held.tile([P, CLASSES // 16], U16, name="offsets")
+        def load_predicted(b):
+            nc.sync.dma_start(predicted[b][:], pre_adj[b * P : (b + 1) * P, :])
+
+        def load_window(b):
+            nc.sync.dma_start(windows[b][:], base[b * P : (b + 1) * P, :])
+
+        load_predicted(0)
+        load_predicted(1)
         nc.sync.dma_start(offsets[:], offs)
+        load_window(0)
+        load_predicted(2)
+        load_predicted(3)
+        for b in range(1, BLOCKS):
+            load_window(b)
 
-        predicted = []
-        windows = []
-        for b in range(BLOCKS):
-            block_rows = slice(b * P, (b + 1) * P)
-            predicted.append(held.tile([P, CLASSES], F32, name=f"predicted{b}"))
-            queue = nc.scalar if b == 0 else nc.sync
-            queue.dma_start(predicted[b][:], pre_adj[block_rows, :])
-            windows.append(held.tile([P, SLOTS], F32, name=f"window{b}"))
-            nc.sync.dma_start(windows[b][:], base[block_rows, :])
-
-        ones = held.tile([P, 1], BF16, name="ones")
-        nc.vector.memset(ones[:], 1.0)
         zeros = held.tile([P, P], BF16, name="zeros")
         nc.vector.memset(zeros[:], 0.0)
+        ones = held.tile([P, 1], BF16, name="ones")
+        nc.vector.memset(ones[:], 1.0)
         minus_half = held.tile([P, 1], F32, name="minus_half")
         nc.vector.memset(minus_half[:], -0.5)
         one = held.tile([P, 1], F32, name="one")
@@ -68,8 +70,8 @@ def tile_adjloss_kernel(tc, base, pre_adj, label, offs, out):
         nc.scalar.activation(table_loaded[:], minus_half[:], ACT.Abs)
 
         def columns(b, part):
-            width = CLASSES // PARTS[b]
-            return slice(part * width, (part + 1) * width)
+            start = sum(WIDTHS[b][:part])
+            return slice(start, start + WIDTHS[b][part])
 
         def block_of_classes(k, b):
             return samples[k // STEPS_PER_LOAD][:, k % STEPS_PER_LOAD, b * P : (b + 1) * P]
@@ -94,11 +96,10 @@ def tile_adjloss_kernel(tc, base, pre_adj, label, offs, out):
                     stop=(b == 0 and k == STEPS - 1),
                 )
 
-        first_width = CLASSES // PARTS[0]
-        first_cooc = [products.tile([P, first_width], F32, name=f"cooc{part}") for part in range(PARTS[0])]
+        first_cooc = [products.tile([P, width], F32, name=f"cooc{part}") for part, width in enumerate(WIDTHS[0])]
         for turn in range(WARM_UP):
             for sums in first_cooc:
-                nc.tensor.matmul(sums[:], zeros[:], zeros[:, 0:first_width], start=(turn == 0), stop=False)
+                nc.tensor.matmul(sums[:], zeros[:], zeros[:], start=(turn == 0), stop=False)
         count_first = counts.tile([P, 1], F32, name="count_first")
         for k in range(EARLY_STEPS):
             add_to_count(count_first, 0, 0, [k])
@@ -140,8 +141,11 @@ def tile_adjloss_kernel(tc, base, pre_adj, label, offs, out):
             )
             nc.scalar.activation(r[:, span], d[:, span], ACT.Abs)
             nc.scalar.activation(r_squared[:, span], d[:, span], ACT.Square)
-            nc.scalar.activation(r_less_half[:, span], r[:, span], ACT.Identity, bias=minus_half[:])
-        for part in range(PARTS[0]):
+            if part < len(first_cooc) // 2:
+                nc.vector.tensor_scalar_sub(r_less_half[:, span], r[:, span], 0.5)
+            else:
+                nc.scalar.activation(r_less_half[:, span], r[:, span], ACT.Identity, bias=minus_half[:])
+        for part in range(len(first_cooc)):
             multiply_by_flag(q, r, r_squared, columns(0, part))
             multiply_by_no_flag(l, r, r_less_half, columns(0, part))
 
@@ -157,8 +161,8 @@ def tile_adjloss_kernel(tc, base, pre_adj, label, offs, out):
 
         def differences(b):
             parts = []
-            for part in range(PARTS[b]):
-                sums = wide_products.tile([P, CLASSES // PARTS[b]], F32, name="sums")
+            for part, width in enumerate(WIDTHS[b]):
+                sums = wide_products.tile([P, width], F32, name="sums")
                 add_products(sums, b, part, range(STEPS))
                 nc.tensor.matmul(
                     sums[:], minus_count_diagonals[b][:], predicted[b][:, columns(b, part)], start=False, stop=True
@@ -172,7 +176,7 @@ def tile_adjloss_kernel(tc, base, pre_adj, label, offs, out):
             parts, inverse_count = differences(b)
             for span, sums in parts:
                 nc.scalar.activation(r[:, span], sums[:], ACT.Abs, scale=inverse_count)
-            nc.scalar.activation(r_squared[:], r[:], ACT.Square)
+                nc.scalar.activation(r_squared[:, span], r[:, span], ACT.Square)
             nc.scalar.activation(r_less_half[:], r[:], ACT.Identity, bias=minus_half[:])
             multiply_by_flag(q, r, r_squared, every_column)
             if b < LAST - 1:

@@ -16,7 +16,7 @@ LAST = BLOCKS - 1
 STEPS = SAMPLES // P
 STEPS_PER_LOAD = 4
 EARLY_STEPS = STEPS_PER_LOAD
-WIDTHS = [[128, 128, 128, 128], [256, 256], [256, 256], [384, 128]]
+WIDTHS = [[128, 128, 128, 128], [128, 384], [512], [384, 128]]
 WARM_UP = 5
 FLOPS = 2 * SAMPLES * CLASSES * CLASSES
 
@@ -112,9 +112,17 @@ def tile_adjloss_kernel(tc, base, pre_adj, label, offs, out):
         for part, sums in enumerate(first_cooc):
             add_products(sums, 0, part, late_steps)
 
+        later_classes = CLASSES - P
+        pair_sums = held.tile([P, 2, later_classes], BF16, name="pair_sums")
+        nc.vector.tensor_tensor(pair_sums[:], samples[0][:, 0:2, P:], samples[0][:, 2:4, P:], ALU.add)
+        early_sums = held.tile([P, later_classes], BF16, name="early_sums")
+        nc.vector.tensor_tensor(early_sums[:], pair_sums[:, 0, :], pair_sums[:, 1, :], ALU.add)
         count_later = counts.tile([P, BLOCKS - 1], F32, name="count_later")
         for b in range(1, BLOCKS):
-            add_to_count(count_later, b - 1, b, range(STEPS))
+            nc.tensor.matmul(
+                count_later[:, b - 1 : b], early_sums[:, (b - 1) * P : b * P], ones[:], start=True, stop=False
+            )
+            add_to_count(count_later, b - 1, b, late_steps)
         inverse_later = held.tile([P, BLOCKS - 1], F32, name="inverse_later")
         nc.vector.reciprocal(inverse_later[:], count_later[:])
 

@@ -115,13 +115,16 @@ def tile_adjloss_kernel(tc, base, pre_adj, label, offs, out):
         later_classes = CLASSES - P
         pair_sums = held.tile([P, 2, later_classes], BF16, name="pair_sums")
         nc.vector.tensor_tensor(pair_sums[:], samples[0][:, 0:2, P:], samples[0][:, 2:4, P:], ALU.add)
-        early_sums = held.tile([P, later_classes], BF16, name="early_sums")
-        nc.vector.tensor_tensor(early_sums[:], pair_sums[:, 0, :], pair_sums[:, 1, :], ALU.add)
         count_later = counts.tile([P, BLOCKS - 1], F32, name="count_later")
         for b in range(1, BLOCKS):
-            nc.tensor.matmul(
-                count_later[:, b - 1 : b], early_sums[:, (b - 1) * P : b * P], ones[:], start=True, stop=False
-            )
+            for pair in range(2):
+                nc.tensor.matmul(
+                    count_later[:, b - 1 : b],
+                    pair_sums[:, pair, (b - 1) * P : b * P],
+                    ones[:],
+                    start=(pair == 0),
+                    stop=False,
+                )
             add_to_count(count_later, b - 1, b, late_steps)
         inverse_later = held.tile([P, BLOCKS - 1], F32, name="inverse_later")
         nc.vector.reciprocal(inverse_later[:], count_later[:])

@@ -47,7 +47,9 @@ def tile_adjloss_kernel(tc, base, pre_adj, label, offs, out):
         def load_window(b):
             nc.sync.dma_start(windows[b][:], base[b * P : (b + 1) * P, :])
 
-        load_predicted(0)
+        for half in range(2):
+            half_columns = slice(half * CLASSES // 2, (half + 1) * CLASSES // 2)
+            nc.sync.dma_start(predicted[0][:, half_columns], pre_adj[0:P, half_columns])
         load_predicted(1)
         nc.sync.dma_start(offsets[:], offs)
         load_window(0)

import concourse.mybir as mybir
from concourse.masks import make_identity

F32 = mybir.dt.float32
BF16 = mybir.dt.bfloat16
U16 = mybir.dt.uint16
ALU = mybir.AluOpType
ACT = mybir.ActivationFunctionType

P = 128
CLASSES = 512
SAMPLES = 1024
SLOTS = 1024
BLOCKS = CLASSES // P
LAST = BLOCKS - 1
STEPS = SAMPLES // P
STEPS_PER_LOAD = 4
EARLY_STEPS = STEPS_PER_LOAD
WIDTHS = [[128, 128, 128, 128], [128, 384], [512], [384, 128]]
WARM_UP = 5
FLOPS = 2 * SAMPLES * CLASSES * CLASSES


def tile_adjloss_kernel(tc, base, pre_adj, label, offs, out):
    nc = tc.nc
    with (
        tc.tile_pool(name="held", bufs=1) as held,
        tc.tile_pool(name="work", bufs=BLOCKS) as work,
        tc.tile_pool(name="handover", bufs=1) as handover,
        tc.psum_pool(name="counts", bufs=1) as counts,
        tc.psum_pool(name="products", bufs=1) as products,
        tc.psum_pool(name="wide_products", bufs=2) as wide_products,
    ):
        label_by_partition = label.rearrange("(p k) c -> p k c", k=STEPS)
        samples = []
        for n in range(STEPS // STEPS_PER_LOAD):
            half = held.tile([P, STEPS_PER_LOAD, CLASSES], BF16, name=f"samples{n}")
            nc.sync.dma_start(half[:], label_by_partition[:, n * STEPS_PER_LOAD : (n + 1) * STEPS_PER_LOAD, :])
            samples.append(half)

        predicted = [held.tile([P, CLASSES], F32, name=f"predicted{b}") for b in range(BLOCKS)]
        windows = [held.tile([P, SLOTS], F32, name=f"window{b}") for b in range(BLOCKS)]
        offsets = held.tile([P, CLASSES // 16], U16, name="offsets")
        def load_predicted(b):
            nc.sync.dma_start(predicted[b][:], pre_adj[b * P : (b + 1) * P, :])

        def load_window(b):
            nc.sync.dma_start(windows[b][:], base[b * P : (b + 1) * P, :])

        for half in range(2):
            half_columns = slice(half * CLASSES // 2, (half + 1) * CLASSES // 2)
            nc.sync.dma_start(predicted[0][:, half_columns], pre_adj[0:P, half_columns])
        load_predicted(1)
        nc.sync.dma_start(offsets[:], offs)
        load_window(0)
        load_predicted(2)
        load_predicted(3)
        for b in range(1, BLOCKS):
            load_window(b)

        zeros = held.tile([P, P], BF16, name="zeros")
        nc.vector.memset(zeros[:], 0.0)
        ones = held.tile([P, 1], BF16, name="ones")
        nc.vector.memset(ones[:], 1.0)
        minus_half = held.tile([P, 1], F32, name="minus_half")
        nc.vector.memset(minus_half[:], -0.5)
        one = held.tile([P, 1], F32, name="one")
        nc.vector.memset(one[:], 1.0)
        identity = held.tile([P, P], F32, name="identity")
        make_identity(nc, identity[:])
        table_loaded = held.tile([P, 1], F32, name="table_loaded")
        nc.scalar.activation(table_loaded[:], minus_half[:], ACT.Abs)

        def columns(b, part):
            start = sum(WIDTHS[b][:part])
            return slice(start, start + WIDTHS[b][part])

        def block_of_classes(k, b):
            return samples[k // STEPS_PER_LOAD][:, k % STEPS_PER_LOAD, b * P : (b + 1) * P]

        def add_to_count(count, column, b, steps):
            for k in steps:
                nc.tensor.matmul(
                    count[:, column : column + 1],
                    block_of_classes(k, b),
                    ones[:],
                    start=(k == 0),
                    stop=(k == STEPS - 1),
                )

        def add_products(sums, b, part, steps):
            for k in steps:
                nc.tensor.matmul(
                    sums[:],
                    block_of_classes(k, b),
                    samples[k // STEPS_PER_LOAD][:, k % STEPS_PER_LOAD, columns(b, part)],
                    start=(b > 0 and k == 0),
                    stop=(b == 0 and k == STEPS - 1),
                )

        first_cooc = [products.tile([P, width], F32, name=f"cooc{part}") for part, width in enumerate(WIDTHS[0])]
        for turn in range(WARM_UP):
            for sums in first_cooc:
                nc.tensor.matmul(sums[:], zeros[:], zeros[:], start=(turn == 0), stop=False)
        count_first = counts.tile([P, 1], F32, name="count_first")
        for k in range(EARLY_STEPS):
            add_to_count(count_first, 0, 0, [k])
            for part, sums in enumerate(first_cooc):
                add_products(sums, 0, part, [k])
        late_steps = range(EARLY_STEPS, STEPS)
        add_to_count(count_first, 0, 0, late_steps)
        inverse_first = held.tile([P, 1], F32, name="inverse_first")
        nc.vector.reciprocal(inverse_first[:], count_first[:])
        for part, sums in enumerate(first_cooc):
            add_products(sums, 0, part, late_steps)

        later_classes = CLASSES - P
        pair_sums = held.tile([P, 2, later_classes], BF16, name="pair_sums")
        nc.vector.tensor_tensor(pair_sums[:], samples[0][:, 0:2, P:], samples[0][:, 2:4, P:], ALU.add)
        count_later = counts.tile([P, BLOCKS - 1], F32, name="count_later")
        for b in range(1, BLOCKS):
            for pair in range(2):
                nc.tensor.matmul(
                    count_later[:, b - 1 : b],
                    pair_sums[:, pair, (b - 1) * P : b * P],
                    ones[:],
                    start=(pair == 0),
                    stop=False,
                )
            add_to_count(count_later, b - 1, b, late_steps)
        inverse_later = held.tile([P, BLOCKS - 1], F32, name="inverse_later")
        nc.vector.reciprocal(inverse_later[:], count_later[:])

        def multiply_by_flag(q, r, r_squared, span):
            nc.vector.scalar_tensor_tensor(q[:, span], r[:, span], 1.0, r_squared[:, span], ALU.is_lt, ALU.mult)

        def multiply_by_no_flag(l, r, r_less_half, span):
            nc.vector.scalar_tensor_tensor(l[:, span], r[:, span], 1.0, r_less_half[:, span], ALU.is_ge, ALU.mult)

        def place(b, q, l):
            nc.vector.tensor_tensor(windows[b][:].indirect(offsets[:]), q[:], l[:], ALU.add)
            nc.sync.dma_start(out[b * P : (b + 1) * P, :], windows[b][:])

        def new_tile(name):
            return work.tile([P, CLASSES], F32, name=name)

        d, r, r_squared, r_less_half, q, l = [
            new_tile(name) for name in ("d", "r", "r_squared", "r_less_half", "q", "l")
        ]
        for part, sums in enumerate(first_cooc):
            span = columns(0, part)
            nc.vector.scalar_tensor_tensor(
                d[:, span], sums[:], inverse_first[:], predicted[0][:, span], ALU.mult, ALU.subtract
            )
            nc.scalar.activation(r[:, span], d[:, span], ACT.Abs)
            nc.scalar.activation(r_squared[:, span], d[:, span], ACT.Square)
            if part < len(first_cooc) // 2:
                nc.vector.tensor_scalar_sub(r_less_half[:, span], r[:, span], 0.5)
            else:
                nc.scalar.activation(r_less_half[:, span], r[:, span], ACT.Identity, bias=minus_half[:])
        for part in range(len(first_cooc)):
            multiply_by_flag(q, r, r_squared, columns(0, part))
            multiply_by_no_flag(l, r, r_less_half, columns(0, part))

        minus_counts = held.tile([P, BLOCKS - 1], F32, name="minus_counts")
        nc.scalar.activation(minus_counts[:], count_later[:], ACT.Copy, scale=-1.0)
        minus_count_diagonals = {}
        for b in range(1, BLOCKS):
            minus_count_diagonals[b] = held.tile([P, P], F32, name=f"minus_count_diagonal{b}")
            nc.scalar.activation(
                minus_count_diagonals[b][:], identity[:], ACT.Identity, scale=minus_counts[:, b - 1 : b]
            )
        place(0, q, l)

        def differences(b):
            parts = []
            for part, width in enumerate(WIDTHS[b]):
                sums = wide_products.tile([P, width], F32, name="sums")
                add_products(sums, b, part, range(STEPS))
                nc.tensor.matmul(
                    sums[:], minus_count_diagonals[b][:], predicted[b][:, columns(b, part)], start=False, stop=True
                )
                parts.append((columns(b, part), sums))
            return parts, inverse_later[:, b - 1 : b]

        every_column = slice(0, CLASSES)
        for b in range(1, LAST):
            r, r_squared, r_less_half, q = [new_tile(name) for name in ("r", "r_squared", "r_less_half", "q")]
            parts, inverse_count = differences(b)
            for span, sums in parts:
                nc.scalar.activation(r[:, span], sums[:], ACT.Abs, scale=inverse_count)
                nc.scalar.activation(r_squared[:, span], r[:, span], ACT.Square)
            nc.scalar.activation(r_less_half[:], r[:], ACT.Identity, bias=minus_half[:])
            multiply_by_flag(q, r, r_squared, every_column)
            if b < LAST - 1:
                l = new_tile("l")
                multiply_by_no_flag(l, r, r_less_half, every_column)
                place(b, q, l)

        r_last = handover.tile([P, CLASSES], F32, name="r_last", tag="handover")
        e = new_tile("e")
        parts, inverse_count = differences(LAST)
        for span, sums in parts:
            nc.scalar.activation(r_last[:, span], sums[:], ACT.Abs, scale=inverse_count)
            nc.vector.scalar_tensor_tensor(e[:, span], r_last[:, span], 1.0, r_last[:, span], ALU.is_lt, ALU.subtract)

        l = handover.tile([P, CLASSES], F32, name="l_before_last", tag="handover")
        multiply_by_no_flag(l, r, r_less_half, every_column)
        place(LAST - 1, q, l)

        size_of_e, flagged_r, q, l = [new_tile(name) for name in ("size_of_e", "flagged_r", "q", "l")]
        nc.scalar.activation(size_of_e[:], e[:], ACT.Abs)
        nc.scalar.activation(flagged_r[:], size_of_e[:], ACT.Relu, scale=-1.0, bias=one[:])
        nc.scalar.activation(q[:], flagged_r[:], ACT.Square)
        nc.scalar.activation(l[:], e[:], ACT.Relu, scale=-1.0, bias=minus_half[:])
        place(LAST, q, l)
